import numpy as np
import ml_dtypes

BF16 = ml_dtypes.bfloat16


def bf(x):
    return np.asarray(x, np.float32).astype(BF16)


def f32(x):
    return np.asarray(x, np.float32)


def f64(x):
    return np.asarray(x).astype(np.float64)


def striped(idx):
    return np.tile(idx.reshape(-1, 16).T, (8, 1))


C, S, K, H, N = 256, 256, 2, 128, 256


def setup_inputs():
    raw = np.random.standard_normal((C, S))
    x = f32(raw * np.sqrt(C) / np.sqrt((raw * raw).sum(axis=0, keepdims=True)))
    o = bf(np.random.standard_normal((C, N)))
    w = bf(np.random.standard_normal((K, C, C)) / np.sqrt(C))
    idx = np.concatenate([np.random.permutation(S)[:H] for _ in range(K)])
    return {"x": x, "o": o, "w": w, "offs": striped(idx)}


def reference(x, o, w, offs):
    idx = offs[:16].T.reshape(-1)
    t = np.concatenate([f64(w)[r].T @ f64(o)[:, r * H:(r + 1) * H] for r in range(K)], axis=1)
    return f64(x)[:, idx] * t

@@ -1,0 +1,52 @@
+import concourse.mybir as mybir
+
+P = 128
+C, K, H, N = 256, 2, 128, 256
+S = 256
+BLOCKS = C // P
+FLOPS = 2 * C * C * N
+
+BF16, F32, U16 = mybir.dt.bfloat16, mybir.dt.float32, mybir.dt.uint16
+MULT = mybir.AluOpType.mult
+COPY = mybir.ActivationFunctionType.Copy
+
+
+def tile_rescal_kernel(tc, x, o, w, offs, out):
+    nc = tc.nc
+    with (
+        tc.tile_pool(name="held", bufs=1) as held,
+        tc.psum_pool(name="psum", bufs=1) as psum,
+    ):
+        offsets = held.tile([P, N // 16], U16, name="offsets")
+        nc.sync.dma_start(offsets[:], offs)
+
+        o_sb = held.tile([P, BLOCKS, N], BF16, name="o_sb")
+        nc.scalar.dma_start(o_sb[:], o.rearrange("(b p) j -> p b j", p=P))
+        w_sb = held.tile([P, K, BLOCKS, C], BF16, name="w_sb")
+        w_queues = (nc.sync, nc.scalar)
+        for r in range(K):
+            w_queues[r].dma_start(w_sb[:, r], w[r].rearrange("(b p) c -> p b c", p=P))
+
+        x_queues = (nc.sync, nc.scalar)
+        x_sb = []
+        for cb in range(BLOCKS):
+            window = held.tile([P, S], F32, name=f"x_sb{cb}")
+            x_queues[cb].dma_start(window[:], x[cb * P:(cb + 1) * P, :])
+            x_sb.append(window)
+
+        for cb in range(BLOCKS):
+            t_ps = psum.tile([P, N], F32, name=f"t_ps{cb}")
+            for r in range(K):
+                for b in range(BLOCKS):
+                    nc.tensor.matmul(
+                        t_ps[:, r * H:(r + 1) * H],
+                        w_sb[:, r, b, cb * P:(cb + 1) * P],
+                        o_sb[:, b, r * H:(r + 1) * H],
+                        start=(b == 0),
+                        stop=(b == BLOCKS - 1),
+                    )
+            t_sb = held.tile([P, N], F32, name=f"t_sb{cb}")
+            nc.scalar.activation(t_sb[:], t_ps[:], COPY)
+            prod = held.tile([P, N], F32, name=f"prod{cb}")
+            nc.vector.tensor_tensor(prod[:], x_sb[cb][:].indirect(offsets[:]), t_sb[:], MULT)
+            x_queues[cb].dma_start(out[cb * P:(cb + 1) * P, :], prod[:])

@@ -17,15 +17,15 @@ def tile_rescal_kernel(tc, x, o, w, offs, out):
         tc.tile_pool(name="held", bufs=1) as held,
         tc.psum_pool(name="psum", bufs=1) as psum,
     ):
-        offsets = held.tile([P, N // 16], U16, name="offsets")
-        nc.sync.dma_start(offsets[:], offs)
-
         o_sb = held.tile([P, BLOCKS, N], BF16, name="o_sb")
-        nc.scalar.dma_start(o_sb[:], o.rearrange("(b p) j -> p b j", p=P))
+        nc.scalar.dma_start(o_sb[:], o.rearrange("(p b) j -> p b j", b=BLOCKS))
         w_sb = held.tile([P, K, BLOCKS, C], BF16, name="w_sb")
         w_queues = (nc.sync, nc.scalar)
         for r in range(K):
-            w_queues[r].dma_start(w_sb[:, r], w[r].rearrange("(b p) c -> p b c", p=P))
+            w_queues[r].dma_start(w_sb[:, r], w[r].rearrange("(p b) c -> p b c", b=BLOCKS))
+
+        offsets = held.tile([P, N // 16], U16, name="offsets")
+        nc.sync.dma_start(offsets[:], offs)
 
         x_queues = (nc.sync, nc.scalar)
         x_sb = []

@@ -15,38 +15,34 @@ def tile_rescal_kernel(tc, x, o, w, offs, out):
     nc = tc.nc
     with (
         tc.tile_pool(name="held", bufs=1) as held,
-        tc.psum_pool(name="psum", bufs=1) as psum,
+        tc.tile_pool(name="work", bufs=K * BLOCKS) as work,
+        tc.psum_pool(name="psum", bufs=K * BLOCKS) as psum,
     ):
         o_sb = held.tile([P, BLOCKS, N], BF16, name="o_sb")
-        nc.scalar.dma_start(o_sb[:], o.rearrange("(p b) j -> p b j", b=BLOCKS))
         w_sb = held.tile([P, K, BLOCKS, C], BF16, name="w_sb")
-        w_queues = (nc.sync, nc.scalar)
-        for r in range(K):
-            w_queues[r].dma_start(w_sb[:, r], w[r].rearrange("(p b) c -> p b c", b=BLOCKS))
-
         offsets = held.tile([P, N // 16], U16, name="offsets")
+        x_sb = [held.tile([P, S], F32, name=f"x_sb{cb}") for cb in range(BLOCKS)]
+
+        nc.sync.dma_start(w_sb[:, 0], w[0].rearrange("(p b) c -> p b c", b=BLOCKS))
+        nc.scalar.dma_start(o_sb[:], o.rearrange("(p b) j -> p b j", b=BLOCKS))
         nc.sync.dma_start(offsets[:], offs)
+        nc.scalar.dma_start(x_sb[0][:], x[0:P, :])
+        nc.sync.dma_start(x_sb[1][:], x[P:2 * P, :])
+        nc.scalar.dma_start(w_sb[:, 1], w[1].rearrange("(p b) c -> p b c", b=BLOCKS))
 
-        x_queues = (nc.sync, nc.scalar)
-        x_sb = []
-        for cb in range(BLOCKS):
-            window = held.tile([P, S], F32, name=f"x_sb{cb}")
-            x_queues[cb].dma_start(window[:], x[cb * P:(cb + 1) * P, :])
-            x_sb.append(window)
-
-        for cb in range(BLOCKS):
-            t_ps = psum.tile([P, N], F32, name=f"t_ps{cb}")
-            for r in range(K):
+        for r in range(K):
+            edges = slice(r * H, (r + 1) * H)
+            for cb in range(BLOCKS):
+                channels = slice(cb * P, (cb + 1) * P)
+                t_ps = psum.tile([P, H], F32, name="t_ps")
                 for b in range(BLOCKS):
                     nc.tensor.matmul(
-                        t_ps[:, r * H:(r + 1) * H],
-                        w_sb[:, r, b, cb * P:(cb + 1) * P],
-                        o_sb[:, b, r * H:(r + 1) * H],
-                        start=(b == 0),
-                        stop=(b == BLOCKS - 1),
+                        t_ps[:], w_sb[:, r, b, channels], o_sb[:, b, edges],
+                        start=(b == 0), stop=(b == BLOCKS - 1),
                     )
-            t_sb = held.tile([P, N], F32, name=f"t_sb{cb}")
-            nc.scalar.activation(t_sb[:], t_ps[:], COPY)
-            prod = held.tile([P, N], F32, name=f"prod{cb}")
-            nc.vector.tensor_tensor(prod[:], x_sb[cb][:].indirect(offsets[:]), t_sb[:], MULT)
-            x_queues[cb].dma_start(out[cb * P:(cb + 1) * P, :], prod[:])
+                t_sb = work.tile([P, H], F32, name="t_sb")
+                nc.scalar.activation(t_sb[:], t_ps[:], COPY)
+                prod = work.tile([P, H], F32, name="prod")
+                picked = x_sb[cb][:].indirect(offsets[:, r * H // 16:(r + 1) * H // 16])
+                nc.vector.tensor_tensor(prod[:], picked, t_sb[:], MULT)
+                nc.sync.dma_start(out[channels, edges], prod[:])

@@ -15,34 +15,36 @@ def tile_rescal_kernel(tc, x, o, w, offs, out):
     nc = tc.nc
     with (
         tc.tile_pool(name="held", bufs=1) as held,
-        tc.tile_pool(name="work", bufs=K * BLOCKS) as work,
-        tc.psum_pool(name="psum", bufs=K * BLOCKS) as psum,
+        tc.psum_pool(name="psum", bufs=1) as psum,
     ):
         o_sb = held.tile([P, BLOCKS, N], BF16, name="o_sb")
         w_sb = held.tile([P, K, BLOCKS, C], BF16, name="w_sb")
         offsets = held.tile([P, N // 16], U16, name="offsets")
         x_sb = [held.tile([P, S], F32, name=f"x_sb{cb}") for cb in range(BLOCKS)]
 
-        nc.sync.dma_start(w_sb[:, 0], w[0].rearrange("(p b) c -> p b c", b=BLOCKS))
-        nc.scalar.dma_start(o_sb[:], o.rearrange("(p b) j -> p b j", b=BLOCKS))
+        o_dram = o.rearrange("(p b) j -> p b j", b=BLOCKS)
+        w_dram = w.rearrange("r (p b) c -> r p b c", b=BLOCKS)
+        nc.sync.dma_start(w_sb[:, 0], w_dram[0])
+        nc.scalar.dma_start(o_sb[:], o_dram)
+        nc.sync.dma_start(w_sb[:, 1, 0], w_dram[1, :, 0])
+        nc.scalar.dma_start(w_sb[:, 1, 1], w_dram[1, :, 1])
         nc.sync.dma_start(offsets[:], offs)
-        nc.scalar.dma_start(x_sb[0][:], x[0:P, :])
-        nc.sync.dma_start(x_sb[1][:], x[P:2 * P, :])
-        nc.scalar.dma_start(w_sb[:, 1], w[1].rearrange("(p b) c -> p b c", b=BLOCKS))
+        nc.sync.dma_start(x_sb[0][:], x[0:P, :])
+        nc.scalar.dma_start(x_sb[1][:], x[P:2 * P, :])
 
-        for r in range(K):
-            edges = slice(r * H, (r + 1) * H)
-            for cb in range(BLOCKS):
-                channels = slice(cb * P, (cb + 1) * P)
-                t_ps = psum.tile([P, H], F32, name="t_ps")
+        store_queues = (nc.sync, nc.scalar)
+        for cb in range(BLOCKS):
+            channels = slice(cb * P, (cb + 1) * P)
+            t_ps = psum.tile([P, N], F32, name=f"t_ps{cb}")
+            for r in range(K):
+                edges = slice(r * H, (r + 1) * H)
                 for b in range(BLOCKS):
                     nc.tensor.matmul(
-                        t_ps[:], w_sb[:, r, b, channels], o_sb[:, b, edges],
+                        t_ps[:, edges], w_sb[:, r, b, channels], o_sb[:, b, edges],
                         start=(b == 0), stop=(b == BLOCKS - 1),
                     )
-                t_sb = work.tile([P, H], F32, name="t_sb")
-                nc.scalar.activation(t_sb[:], t_ps[:], COPY)
-                prod = work.tile([P, H], F32, name="prod")
-                picked = x_sb[cb][:].indirect(offsets[:, r * H // 16:(r + 1) * H // 16])
-                nc.vector.tensor_tensor(prod[:], picked, t_sb[:], MULT)
-                nc.sync.dma_start(out[channels, edges], prod[:])
+            t_sb = held.tile([P, N], F32, name=f"t_sb{cb}")
+            nc.scalar.activation(t_sb[:], t_ps[:], COPY)
+            prod = held.tile([P, N], F32, name=f"prod{cb}")
+            nc.vector.tensor_tensor(prod[:], x_sb[cb][:].indirect(offsets[:]), t_sb[:], MULT)
+            store_queues[cb].dma_start(out[channels, :], prod[:])

@@ -22,15 +22,11 @@ def tile_rescal_kernel(tc, x, o, w, offs, out):
         offsets = held.tile([P, N // 16], U16, name="offsets")
         x_sb = [held.tile([P, S], F32, name=f"x_sb{cb}") for cb in range(BLOCKS)]
 
-        o_dram = o.rearrange("(p b) j -> p b j", b=BLOCKS)
-        w_dram = w.rearrange("r (p b) c -> r p b c", b=BLOCKS)
-        nc.sync.dma_start(w_sb[:, 0], w_dram[0])
-        nc.scalar.dma_start(o_sb[:], o_dram)
-        nc.sync.dma_start(w_sb[:, 1, 0], w_dram[1, :, 0])
-        nc.scalar.dma_start(w_sb[:, 1, 1], w_dram[1, :, 1])
+        nc.sync.dma_start(w_sb[:], w.rearrange("r (p b) c -> p r b c", b=BLOCKS))
+        nc.scalar.dma_start(o_sb[:], o.rearrange("(p b) j -> p b j", b=BLOCKS))
         nc.sync.dma_start(offsets[:], offs)
-        nc.sync.dma_start(x_sb[0][:], x[0:P, :])
-        nc.scalar.dma_start(x_sb[1][:], x[P:2 * P, :])
+        nc.scalar.dma_start(x_sb[0][:], x[0:P, :])
+        nc.sync.dma_start(x_sb[1][:], x[P:2 * P, :])
 
         store_queues = (nc.sync, nc.scalar)
         for cb in range(BLOCKS):

@@ -22,13 +22,14 @@ def tile_rescal_kernel(tc, x, o, w, offs, out):
         offsets = held.tile([P, N // 16], U16, name="offsets")
         x_sb = [held.tile([P, S], F32, name=f"x_sb{cb}") for cb in range(BLOCKS)]
 
-        nc.sync.dma_start(w_sb[:], w.rearrange("r (p b) c -> p r b c", b=BLOCKS))
+        nc.sync.dma_start(w_sb[:, 0], w[0].rearrange("(p b) c -> p b c", b=BLOCKS))
         nc.scalar.dma_start(o_sb[:], o.rearrange("(p b) j -> p b j", b=BLOCKS))
+        nc.scalar.dma_start(w_sb[:, 1], w[1].rearrange("(p b) c -> p b c", b=BLOCKS))
         nc.sync.dma_start(offsets[:], offs)
-        nc.scalar.dma_start(x_sb[0][:], x[0:P, :])
-        nc.sync.dma_start(x_sb[1][:], x[P:2 * P, :])
+        nc.sync.dma_start(x_sb[0][:], x[0:P, :])
+        nc.scalar.dma_start(x_sb[1][:], x[P:2 * P, :])
 
-        store_queues = (nc.sync, nc.scalar)
+        t_sb = []
         for cb in range(BLOCKS):
             channels = slice(cb * P, (cb + 1) * P)
             t_ps = psum.tile([P, N], F32, name=f"t_ps{cb}")
@@ -39,8 +40,14 @@ def tile_rescal_kernel(tc, x, o, w, offs, out):
                         t_ps[:, edges], w_sb[:, r, b, channels], o_sb[:, b, edges],
                         start=(b == 0), stop=(b == BLOCKS - 1),
                     )
-            t_sb = held.tile([P, N], F32, name=f"t_sb{cb}")
-            nc.scalar.activation(t_sb[:], t_ps[:], COPY)
+            t_sb.append(held.tile([P, N], F32, name=f"t_sb{cb}"))
+            nc.scalar.activation(t_sb[cb][:], t_ps[:], COPY)
+
+        store_queues = (nc.sync, nc.scalar)
+        for cb in range(BLOCKS):
+            channels = slice(cb * P, (cb + 1) * P)
             prod = held.tile([P, N], F32, name=f"prod{cb}")
-            nc.vector.tensor_tensor(prod[:], x_sb[cb][:].indirect(offsets[:]), t_sb[:], MULT)
-            store_queues[cb].dma_start(out[channels, :], prod[:])
+            nc.vector.tensor_tensor(prod[:], x_sb[cb][:].indirect(offsets[:]), t_sb[cb][:], MULT)
+            for r in range(K):
+                edges = slice(r * H, (r + 1) * H)
+                store_queues[r].dma_start(out[channels, edges], prod[:, edges])

@@ -15,7 +15,8 @@ def tile_rescal_kernel(tc, x, o, w, offs, out):
     nc = tc.nc
     with (
         tc.tile_pool(name="held", bufs=1) as held,
-        tc.psum_pool(name="psum", bufs=1) as psum,
+        tc.tile_pool(name="work", bufs=K * BLOCKS) as work,
+        tc.psum_pool(name="psum", bufs=K * BLOCKS) as psum,
     ):
         o_sb = held.tile([P, BLOCKS, N], BF16, name="o_sb")
         w_sb = held.tile([P, K, BLOCKS, C], BF16, name="w_sb")
@@ -29,25 +30,20 @@ def tile_rescal_kernel(tc, x, o, w, offs, out):
         nc.sync.dma_start(x_sb[0][:], x[0:P, :])
         nc.scalar.dma_start(x_sb[1][:], x[P:2 * P, :])
 
-        t_sb = []
-        for cb in range(BLOCKS):
-            channels = slice(cb * P, (cb + 1) * P)
-            t_ps = psum.tile([P, N], F32, name=f"t_ps{cb}")
-            for r in range(K):
-                edges = slice(r * H, (r + 1) * H)
-                for b in range(BLOCKS):
-                    nc.tensor.matmul(
-                        t_ps[:, edges], w_sb[:, r, b, channels], o_sb[:, b, edges],
-                        start=(b == 0), stop=(b == BLOCKS - 1),
-                    )
-            t_sb.append(held.tile([P, N], F32, name=f"t_sb{cb}"))
-            nc.scalar.activation(t_sb[cb][:], t_ps[:], COPY)
-
         store_queues = (nc.sync, nc.scalar)
         for cb in range(BLOCKS):
             channels = slice(cb * P, (cb + 1) * P)
             prod = held.tile([P, N], F32, name=f"prod{cb}")
-            nc.vector.tensor_tensor(prod[:], x_sb[cb][:].indirect(offsets[:]), t_sb[cb][:], MULT)
             for r in range(K):
                 edges = slice(r * H, (r + 1) * H)
-                store_queues[r].dma_start(out[channels, edges], prod[:, edges])
+                t_ps = psum.tile([P, H], F32, name="t_ps")
+                for b in range(BLOCKS):
+                    nc.tensor.matmul(
+                        t_ps[:], w_sb[:, r, b, channels], o_sb[:, b, edges],
+                        start=(b == 0), stop=(b == BLOCKS - 1),
+                    )
+                t_sb = work.tile([P, H], F32, name="t_sb")
+                nc.scalar.activation(t_sb[:], t_ps[:], COPY)
+                picked = x_sb[cb][:].indirect(offsets[:, r * H // 16:(r + 1) * H // 16])
+                nc.vector.tensor_tensor(prod[:, edges], picked, t_sb[:], MULT)
+            store_queues[cb].dma_start(out[channels, :], prod[:])

@@ -31,11 +31,11 @@ def tile_rescal_kernel(tc, x, o, w, offs, out):
         nc.scalar.dma_start(x_sb[1][:], x[P:2 * P, :])
 
         store_queues = (nc.sync, nc.scalar)
-        for cb in range(BLOCKS):
-            channels = slice(cb * P, (cb + 1) * P)
-            prod = held.tile([P, N], F32, name=f"prod{cb}")
-            for r in range(K):
-                edges = slice(r * H, (r + 1) * H)
+        prod = [held.tile([P, N], F32, name=f"prod{cb}") for cb in range(BLOCKS)]
+        for r in range(K):
+            edges = slice(r * H, (r + 1) * H)
+            for cb in range(BLOCKS):
+                channels = slice(cb * P, (cb + 1) * P)
                 t_ps = psum.tile([P, H], F32, name="t_ps")
                 for b in range(BLOCKS):
                     nc.tensor.matmul(
@@ -45,5 +45,6 @@ def tile_rescal_kernel(tc, x, o, w, offs, out):
                 t_sb = work.tile([P, H], F32, name="t_sb")
                 nc.scalar.activation(t_sb[:], t_ps[:], COPY)
                 picked = x_sb[cb][:].indirect(offsets[:, r * H // 16:(r + 1) * H // 16])
-                nc.vector.tensor_tensor(prod[:, edges], picked, t_sb[:], MULT)
-            store_queues[cb].dma_start(out[channels, :], prod[:])
+                nc.vector.tensor_tensor(prod[cb][:, edges], picked, t_sb[:], MULT)
+        for cb in range(BLOCKS):
+            store_queues[cb].dma_start(out[cb * P:(cb + 1) * P, :], prod[cb][:])

@@ -31,9 +31,10 @@ def tile_rescal_kernel(tc, x, o, w, offs, out):
         nc.scalar.dma_start(x_sb[1][:], x[P:2 * P, :])
 
         store_queues = (nc.sync, nc.scalar)
-        prod = [held.tile([P, N], F32, name=f"prod{cb}") for cb in range(BLOCKS)]
+        out_blocks = out.rearrange("(cb p) j -> p cb j", p=P)
         for r in range(K):
             edges = slice(r * H, (r + 1) * H)
+            prod = held.tile([P, BLOCKS, H], F32, name=f"prod{r}")
             for cb in range(BLOCKS):
                 channels = slice(cb * P, (cb + 1) * P)
                 t_ps = psum.tile([P, H], F32, name="t_ps")
@@ -45,6 +46,5 @@ def tile_rescal_kernel(tc, x, o, w, offs, out):
                 t_sb = work.tile([P, H], F32, name="t_sb")
                 nc.scalar.activation(t_sb[:], t_ps[:], COPY)
                 picked = x_sb[cb][:].indirect(offsets[:, r * H // 16:(r + 1) * H // 16])
-                nc.vector.tensor_tensor(prod[cb][:, edges], picked, t_sb[:], MULT)
-        for cb in range(BLOCKS):
-            store_queues[cb].dma_start(out[cb * P:(cb + 1) * P, :], prod[cb][:])
+                nc.vector.tensor_tensor(prod[:, cb, :], picked, t_sb[:], MULT)
+            store_queues[r].dma_start(out_blocks[:, :, edges], prod[:])

@@ -30,7 +30,7 @@ def tile_rescal_kernel(tc, x, o, w, offs, out):
         nc.sync.dma_start(x_sb[0][:], x[0:P, :])
         nc.scalar.dma_start(x_sb[1][:], x[P:2 * P, :])
 
-        store_queues = (nc.sync, nc.scalar)
+        store_queues = (nc.scalar, nc.sync)
         out_blocks = out.rearrange("(cb p) j -> p cb j", p=P)
         for r in range(K):
             edges = slice(r * H, (r + 1) * H)

import concourse.mybir as mybir

P = 128
C, K, H, N = 256, 2, 128, 256
S = 256
BLOCKS = C // P
FLOPS = 2 * C * C * N

BF16, F32, U16 = mybir.dt.bfloat16, mybir.dt.float32, mybir.dt.uint16
MULT = mybir.AluOpType.mult
COPY = mybir.ActivationFunctionType.Copy


def tile_rescal_kernel(tc, x, o, w, offs, out):
    nc = tc.nc
    with (
        tc.tile_pool(name="held", bufs=1) as held,
        tc.tile_pool(name="work", bufs=K * BLOCKS) as work,
        tc.psum_pool(name="psum", bufs=K * BLOCKS) as psum,
    ):
        o_sb = held.tile([P, BLOCKS, N], BF16, name="o_sb")
        w_sb = held.tile([P, K, BLOCKS, C], BF16, name="w_sb")
        offsets = held.tile([P, N // 16], U16, name="offsets")
        x_sb = [held.tile([P, S], F32, name=f"x_sb{cb}") for cb in range(BLOCKS)]

        nc.sync.dma_start(w_sb[:, 0], w[0].rearrange("(p b) c -> p b c", b=BLOCKS))
        nc.scalar.dma_start(o_sb[:], o.rearrange("(p b) j -> p b j", b=BLOCKS))
        nc.scalar.dma_start(w_sb[:, 1], w[1].rearrange("(p b) c -> p b c", b=BLOCKS))
        nc.sync.dma_start(offsets[:], offs)
        nc.sync.dma_start(x_sb[0][:], x[0:P, :])
        nc.scalar.dma_start(x_sb[1][:], x[P:2 * P, :])

        store_queues = (nc.scalar, nc.sync)
        out_blocks = out.rearrange("(cb p) j -> p cb j", p=P)
        for r in range(K):
            edges = slice(r * H, (r + 1) * H)
            prod = held.tile([P, BLOCKS, H], F32, name=f"prod{r}")
            for cb in range(BLOCKS):
                channels = slice(cb * P, (cb + 1) * P)
                t_ps = psum.tile([P, H], F32, name="t_ps")
                for b in range(BLOCKS):
                    nc.tensor.matmul(
                        t_ps[:], w_sb[:, r, b, channels], o_sb[:, b, edges],
                        start=(b == 0), stop=(b == BLOCKS - 1),
                    )
                t_sb = work.tile([P, H], F32, name="t_sb")
                nc.scalar.activation(t_sb[:], t_ps[:], COPY)
                picked = x_sb[cb][:].indirect(offsets[:, r * H // 16:(r + 1) * H // 16])
                nc.vector.tensor_tensor(prod[:, cb, :], picked, t_sb[:], MULT)
            store_queues[r].dma_start(out_blocks[:, :, edges], prod[:])
